import numpy as np
import ml_dtypes


def mxq(x, axis, fmt="e4m3"):
    dtype, down = {"e4m3": (ml_dtypes.float8_e4m3fn, 7), "e5m2": (ml_dtypes.float8_e5m2, 14)}[fmt]
    v = np.moveaxis(np.asarray(x, np.float32).astype(ml_dtypes.bfloat16).astype(np.float64), axis, -1)
    blocks = v.reshape(v.shape[:-1] + (-1, 32))
    amax = np.abs(blocks).max(-1, keepdims=True)
    byte = np.maximum(np.where(amax > 0, np.frexp(amax)[1] - 1 + 127, 0) - down, 1)
    scale = np.exp2(byte - 127.0)
    codes = (blocks / scale).astype(np.float32).astype(dtype).astype(np.float64)
    return np.moveaxis((codes * scale).reshape(v.shape), -1, axis)


WIDE = False


def mx_kscale(k):
    if not WIDE:
        return np.ones(k)
    levels = np.array([10, -10, 5, -5, 0])
    if k % 512:
        return np.exp2(np.random.permutation(np.resize(levels, k // 32))).repeat(32)
    a = np.empty((k // 512, 16))
    for p in range(k // 512):
        a[p, :8] = np.random.permutation(np.resize(levels, 8))
        for g in range(8):
            far = levels[np.abs(levels - a[p, g]) >= 10]
            a[p, g + 8] = far[np.random.randint(len(far))]
    return np.exp2(a.ravel()).repeat(32)


BF16 = ml_dtypes.bfloat16


def bf(x):
    return np.asarray(x, np.float32).astype(BF16)


def f64(x):
    return np.asarray(x).astype(np.float64)


B, IDIM, HDIM, ODIM, S, DEPTH, NACT, NTOP = 128, 512, 512, 128, 128, 32, 3, 2


def sigmoid(v):
    return 1.0 / (1.0 + np.exp(-v))


def setup_inputs():
    s = mx_kscale(HDIM)
    return {"h": bf(sigmoid(np.random.standard_normal((B, HDIM)) * 1.3) * s),
            "stack": bf(np.random.standard_normal((B, DEPTH, S))),
            "Wa": bf(np.random.standard_normal((NACT * S, HDIM)) * 3.0 / np.sqrt(HDIM) / s),
            "ba": bf(np.random.standard_normal(NACT * S) * 0.5),
            "Ws": bf(np.random.standard_normal((S, HDIM)) * 2.0 / np.sqrt(HDIM) / s),
            "bs": bf(np.random.standard_normal(S)),
            "Wo": bf(np.random.standard_normal((ODIM, HDIM)) * 2.0 / np.sqrt(HDIM) / s),
            "bo": bf(np.random.standard_normal(ODIM) * 0.3)}


def reference(h, stack, Wa, ba, Ws, bs, Wo, bo):
    st = f64(stack)
    hq = mxq(f64(h), 1, "e4m3")
    logits = ((hq @ mxq(f64(Wa), 1, "e4m3").T) + f64(ba)).reshape(-1, NACT, S)
    e = np.exp(logits - logits.max(axis=1, keepdims=True))
    act = e / e.sum(axis=1, keepdims=True)
    top = sigmoid((hq @ mxq(f64(Ws), 1, "e4m3").T) + f64(bs))[:, None, :]
    push = np.concatenate([top, st[:, :-1]], axis=1)
    empty = np.full((st.shape[0], 1, S), -1.0)
    pop = np.concatenate([st[:, 1:], empty], axis=1)
    new_stack = (push * act[:, 0][:, None, :]
                 + pop * act[:, 1][:, None, :]
                 + st * act[:, 2][:, None, :])
    out = (hq @ mxq(f64(Wo), 1, "e4m3").T) + f64(bo)
    return out, new_stack

@@ -1,0 +1,263 @@
+from contextlib import ExitStack
+
+import concourse.masks as masks
+import concourse.mybir as mybir
+
+F32 = mybir.dt.float32
+BF16 = mybir.dt.bfloat16
+U32 = mybir.dt.uint32
+U8 = mybir.dt.uint8
+FP8X4 = mybir.dt.float8_e4m3fn_x4
+ACT = mybir.ActivationFunctionType
+ALU = mybir.AluOpType
+AXIS = mybir.AxisListType
+
+P = 128
+HDIM = 512
+DEPTH = 32
+HALVES = 2
+PACK = 4
+
+H_BLOCK = 0
+PUSH, POP, NOOP, TOP, OUT = 0, 1, 2, 3, 4
+OPERANDS = 6
+
+PSUM_BANKS = 8
+SLICES_PER_BANK = 8
+STACK_BANKS = DEPTH // SLICES_PER_BANK
+CHUNK = 4
+TAIL = 2
+STEPS = DEPTH + 1
+AHEAD = 6
+
+FLOPS = 2 * P * HDIM * (3 * P + P + P)
+
+
+def tile_stackrnn_pb_s_kernel(tc, h, stack, Wa, ba, Ws, bs, Wo, bo, out_0, out_1):
+    nc = tc.nc
+    with ExitStack() as ctx:
+        keep = ctx.enter_context(tc.tile_pool(name="keep", bufs=1))
+        staging = ctx.enter_context(tc.tile_pool(name="staging", bufs=4))
+        psum = ctx.enter_context(tc.psum_pool(name="psum", bufs=PSUM_BANKS))
+
+        operands = keep.tile([P, OPERANDS, HDIM], BF16)
+        nc.sync.dma_start(out=operands[:, H_BLOCK, :], in_=h)
+        for j in (PUSH, POP, NOOP):
+            nc.sync.dma_start(out=operands[:, 1 + j, :], in_=Wa[j * P : (j + 1) * P, :])
+        nc.sync.dma_start(out=operands[:, 1 + TOP, :], in_=Ws)
+        nc.sync.dma_start(out=operands[:, 1 + OUT, :], in_=Wo)
+        stack_sb = keep.tile([P, DEPTH, P], BF16)
+        for bank in range(STACK_BANKS):
+            d_range = slice(bank * SLICES_PER_BANK, (bank + 1) * SLICES_PER_BANK)
+            nc.sync.dma_start(out=stack_sb[:, d_range, :], in_=stack[:, d_range, :])
+
+        bias_rows = keep.tile([P, P], BF16)
+        nc.vector.memset(bias_rows[:], 0.0)
+        nc.scalar.dma_start(out=bias_rows[PUSH : NOOP + 1, :], in_=ba.rearrange("(j n) -> j n", n=P))
+        nc.scalar.dma_start(out=bias_rows[TOP : TOP + 1, :], in_=bs.rearrange("(o n) -> o n", o=1))
+        nc.scalar.dma_start(out=bias_rows[OUT : OUT + 1, :], in_=bo.rearrange("(o n) -> o n", o=1))
+
+        warm = keep.tile([P, 1], F32)
+        nc.vector.memset(warm[:], 0.0)
+        nc.scalar.activation(out=warm[:], in_=warm[:], func=ACT.Exp)
+
+        ident_f32 = keep.tile([P, P], F32)
+        masks.make_identity(nc, ident_f32[:])
+        ident_bf16 = keep.tile([P, P], BF16)
+        masks.make_identity(nc, ident_bf16[:])
+
+        rows = keep.tile([P, DEPTH + 2, P], F32)
+        nc.gpsimd.memset(rows[:, DEPTH + 1, :], -1.0)
+        step = keep.tile([P, STEPS, P], F32)
+
+        grouped = keep.tile([P, OPERANDS, P, PACK], BF16, align_bytes=64)
+        grouped_words = grouped[:].bitcast(F32)
+        codes = keep.tile([P, OPERANDS * P], U32, align_bytes=64)
+        scales = keep.tile([P, OPERANDS * P], U8, align_bytes=64)
+
+        def turn_pair(pair):
+            turned = psum.tile([P, 2, HALVES, P], F32, tag="bank")
+            for i in range(2):
+                words = operands[:, 2 * pair + i, :].bitcast(F32)
+                for u in range(HALVES):
+                    nc.tensor.transpose(
+                        out=turned[:, i, u, :], in_=words[:, u : HALVES * P : HALVES], identity=ident_f32[:]
+                    )
+            copy_out = nc.scalar.copy if pair % 2 == 0 else nc.vector.tensor_copy
+            copy_out(
+                out=grouped_words[:, 2 * pair : 2 * pair + 2, :, :],
+                in_=turned[:].rearrange("p i u r -> p i r u"),
+            )
+
+        def quantise_pair(pair):
+            cols = slice(2 * pair * P, (2 * pair + 2) * P)
+            nc.vector.quantize_mx(
+                out=codes[:, cols].bitcast(FP8X4),
+                scales=scales[:, cols],
+                in_=grouped[:, 2 * pair : 2 * pair + 2, :, :].rearrange("p o r t -> p (o r t)"),
+            )
+
+        turn_pair(0)
+        turn_pair(1)
+        quantise_pair(0)
+        bias_turned = psum.tile([P, P], BF16, tag="bank")
+        nc.tensor.transpose(out=bias_turned[:], in_=bias_rows[:], identity=ident_bf16[:])
+        bias = keep.tile([P, OUT + 1], F32)
+        nc.vector.tensor_copy(out=bias[:], in_=bias_turned[:, 0 : OUT + 1])
+        half_bs = keep.tile([P, 1], F32)
+        nc.vector.tensor_scalar_mul(out=half_bs[:], in0=bias[:, TOP : TOP + 1], scalar1=0.5)
+        quantise_pair(1)
+        turn_pair(2)
+        quantise_pair(2)
+
+        gates = psum.tile([P, TOP + 1, P], F32, tag="bank")
+        readout = psum.tile([P, P], F32, tag="bank")
+        h_cols = slice(H_BLOCK * P, (H_BLOCK + 1) * P)
+        for j in range(OUT + 1):
+            w_cols = slice((1 + j) * P, (2 + j) * P)
+            nc.tensor.matmul_mx(
+                out=readout[:] if j == OUT else gates[:, j, :],
+                lhsT=codes[:, w_cols].bitcast(FP8X4),
+                lhsT_scale=scales[:, w_cols],
+                rhs=codes[:, h_cols].bitcast(FP8X4),
+                rhs_scale=scales[:, h_cols],
+                start=True,
+                stop=True,
+            )
+
+        half_tanh = keep.tile([P, P], F32)
+        nc.scalar.activation(
+            out=half_tanh[:], in_=gates[:, TOP, :], func=ACT.Tanh, bias=half_bs[:], scale=0.5
+        )
+        nc.scalar.activation(out=rows[:, 0, :], in_=half_tanh[:], func=ACT.Copy, bias=0.5, scale=0.5)
+        out_turned = keep.tile([P, P], F32)
+        nc.scalar.activation(
+            out=out_turned[:], in_=readout[:], func=ACT.Identity, bias=bias[:, OUT : OUT + 1]
+        )
+
+        stack_turned = []
+        for bank in range(STACK_BANKS):
+            turned_bank = psum.tile([P, SLICES_PER_BANK, P], BF16, tag="bank", name="stack_turned%d" % bank)
+            for i in range(SLICES_PER_BANK):
+                nc.tensor.transpose(
+                    out=turned_bank[:, i, :],
+                    in_=stack_sb[:, bank * SLICES_PER_BANK + i, :],
+                    identity=ident_bf16[:],
+                )
+            stack_turned.append(turned_bank)
+
+        def widen_bank(bank):
+            first = 1 + bank * SLICES_PER_BANK
+            nc.scalar.copy(out=rows[:, first : first + SLICES_PER_BANK, :], in_=stack_turned[bank][:])
+
+        def make_steps(piece):
+            lo = piece * CHUNK
+            hi = min(lo + CHUNK, STEPS)
+            nc.vector.tensor_sub(out=step[:, lo:hi, :], in0=rows[:, lo + 1 : hi + 1, :], in1=rows[:, lo:hi, :])
+
+        out_bank = psum.tile([P, P], F32, tag="bank")
+        nc.tensor.transpose(out=out_bank[:], in_=out_turned[:], identity=ident_f32[:])
+
+        chunks = [(first, CHUNK) for first in range(0, DEPTH - CHUNK, CHUNK)]
+        chunks += [(DEPTH - CHUNK, TAIL), (DEPTH - TAIL, TAIL)]
+        blended = []
+
+        def turn_back(bank, term, first_of_group, last_of_group):
+            count = term.shape[1]
+            for i in range(count):
+                nc.tensor.matmul(
+                    out=bank[:, i, :],
+                    lhsT=term[:, i, :],
+                    rhs=ident_f32[:],
+                    is_transpose=True,
+                    start=(first_of_group and i == 0),
+                    stop=(last_of_group and i == count - 1),
+                )
+
+        def open_chunk(n):
+            first, count = chunks[n]
+            blended.append(psum.tile([P, count, P], F32, tag="bank", name="blended%d" % n))
+            turn_back(blended[n], rows[:, first + 1 : first + 1 + count, :], True, False)
+
+        halves = (slice(0, P // 2), slice(P // 2, P))
+        logits = keep.tile([P, 3, P], F32)
+        for cols in halves:
+            nc.vector.tensor_tensor(
+                out=logits[:, :, cols],
+                in0=gates[:, PUSH : NOOP + 1, cols],
+                in1=bias[:, PUSH : NOOP + 1].unsqueeze(2).to_broadcast([P, 3, P // 2]),
+                op=ALU.add,
+            )
+        peak = keep.tile([P, P], F32)
+        for cols in halves:
+            nc.vector.tensor_reduce(
+                out=peak[:, cols], in_=logits[:, :, cols].rearrange("p j b -> p b j"), axis=AXIS.X, op=ALU.max
+            )
+        for cols in halves:
+            nc.vector.tensor_tensor(
+                out=logits[:, :, cols],
+                in0=logits[:, :, cols],
+                in1=peak[:, cols].unsqueeze(1).to_broadcast([P, 3, P // 2]),
+                op=ALU.subtract,
+            )
+        widen_bank(0)
+        raised = keep.tile([P, 3, P], F32)
+        for cols in halves:
+            nc.scalar.activation(out=raised[:, :, cols], in_=logits[:, :, cols], func=ACT.Exp)
+        widen_bank(1)
+        out_sb = keep.tile([P, P], F32)
+        nc.scalar.copy(out=out_sb[:], in_=out_bank[:])
+        nc.sync.dma_start(out=out_0, in_=out_sb[:])
+        widen_bank(2)
+        widen_bank(3)
+        for n in range(AHEAD):
+            open_chunk(n)
+
+        make_steps(0)
+        make_steps(1)
+        total = keep.tile([P, P], F32)
+        for cols in halves:
+            nc.vector.tensor_reduce(
+                out=total[:, cols], in_=raised[:, :, cols].rearrange("p j b -> p b j"), axis=AXIS.X, op=ALU.add
+            )
+        for cols in halves:
+            nc.vector.reciprocal(out=total[:, cols], in_=total[:, cols])
+        minus_push = keep.tile([P, P], F32)
+        for cols in halves:
+            nc.vector.scalar_tensor_tensor(
+                out=minus_push[:, cols],
+                in0=raised[:, PUSH, cols],
+                scalar=-1.0,
+                in1=total[:, cols],
+                op0=ALU.mult,
+                op1=ALU.mult,
+            )
+        pop = keep.tile([P, P], F32)
+        for cols in halves:
+            nc.vector.tensor_mul(out=pop[:, cols], in0=raised[:, POP, cols], in1=total[:, cols])
+
+        pushed = keep.tile([P, DEPTH, P], F32)
+        popped = keep.tile([P, DEPTH, P], F32)
+        for n, (first, count) in enumerate(chunks):
+            d_range = slice(first, first + count)
+            if (n + 2) * CHUNK < STEPS:
+                make_steps(n + 2)
+            nc.vector.tensor_tensor(
+                out=pushed[:, d_range, :],
+                in0=step[:, d_range, :],
+                in1=minus_push[:].unsqueeze(1).to_broadcast([P, count, P]),
+                op=ALU.mult,
+            )
+            nc.vector.tensor_tensor(
+                out=popped[:, d_range, :],
+                in0=step[:, first + 1 : first + 1 + count, :],
+                in1=pop[:].unsqueeze(1).to_broadcast([P, count, P]),
+                op=ALU.mult,
+            )
+            turn_back(blended[n], pushed[:, d_range, :], False, False)
+            turn_back(blended[n], popped[:, d_range, :], False, True)
+            if n + AHEAD < len(chunks):
+                open_chunk(n + AHEAD)
+            new_rows = staging.tile([P, count, P], F32, tag="new_rows")
+            nc.scalar.copy(out=new_rows[:], in_=blended[n][:])
+            nc.sync.dma_start(out=out_1[:, d_range, :], in_=new_rows[:])

@@ -23,12 +23,10 @@ PUSH, POP, NOOP, TOP, OUT = 0, 1, 2, 3, 4
 OPERANDS = 6
 
 PSUM_BANKS = 8
-SLICES_PER_BANK = 8
-STACK_BANKS = DEPTH // SLICES_PER_BANK
-CHUNK = 4
-TAIL = 2
-STEPS = DEPTH + 1
-AHEAD = 6
+BANK_ROWS = 8
+STACK_BANKS = DEPTH // BANK_ROWS
+GROUP = 4
+WARM_UP = 8
 
 FLOPS = 2 * P * HDIM * (3 * P + P + P)
 
@@ -39,84 +37,76 @@ def tile_stackrnn_pb_s_kernel(tc, h, stack, Wa, ba, Ws, bs, Wo, bo, out_0, out_1
         keep = ctx.enter_context(tc.tile_pool(name="keep", bufs=1))
         staging = ctx.enter_context(tc.tile_pool(name="staging", bufs=4))
         psum = ctx.enter_context(tc.psum_pool(name="psum", bufs=PSUM_BANKS))
+        ctx.enter_context(tc.manual_schedule())
+
+        ba_rows = keep.tile([P, 3, P], BF16)
+        nc.vector.memset(ba_rows[:], 0.0)
+        bso_rows = keep.tile([P, P], BF16)
+        nc.vector.memset(bso_rows[:], 0.0)
+
+        warm = keep.tile([P, 1], F32)
+        nc.vector.memset(warm[:], 0.0)
+        nc.scalar.activation(out=warm[:], in_=warm[:], func=ACT.Exp)
 
         operands = keep.tile([P, OPERANDS, HDIM], BF16)
         nc.sync.dma_start(out=operands[:, H_BLOCK, :], in_=h)
         for j in (PUSH, POP, NOOP):
             nc.sync.dma_start(out=operands[:, 1 + j, :], in_=Wa[j * P : (j + 1) * P, :])
+        nc.sync.dma_start(out=ba_rows[0:1, :, :], in_=ba.rearrange("(o j n) -> o j n", o=1, n=P))
         nc.sync.dma_start(out=operands[:, 1 + TOP, :], in_=Ws)
         nc.sync.dma_start(out=operands[:, 1 + OUT, :], in_=Wo)
         stack_sb = keep.tile([P, DEPTH, P], BF16)
-        for bank in range(STACK_BANKS):
-            d_range = slice(bank * SLICES_PER_BANK, (bank + 1) * SLICES_PER_BANK)
+
+        def load_stack(bank):
+            d_range = slice(bank * BANK_ROWS, (bank + 1) * BANK_ROWS)
             nc.sync.dma_start(out=stack_sb[:, d_range, :], in_=stack[:, d_range, :])
 
-        bias_rows = keep.tile([P, P], BF16)
-        nc.vector.memset(bias_rows[:], 0.0)
-        nc.scalar.dma_start(out=bias_rows[PUSH : NOOP + 1, :], in_=ba.rearrange("(j n) -> j n", n=P))
-        nc.scalar.dma_start(out=bias_rows[TOP : TOP + 1, :], in_=bs.rearrange("(o n) -> o n", o=1))
-        nc.scalar.dma_start(out=bias_rows[OUT : OUT + 1, :], in_=bo.rearrange("(o n) -> o n", o=1))
-
-        warm = keep.tile([P, 1], F32)
-        nc.vector.memset(warm[:], 0.0)
-        nc.scalar.activation(out=warm[:], in_=warm[:], func=ACT.Exp)
+        load_stack(0)
+        nc.sync.dma_start(out=bso_rows[0:1, :], in_=bs.rearrange("(o n) -> o n", o=1))
+        nc.sync.dma_start(out=bso_rows[1:2, :], in_=bo.rearrange("(o n) -> o n", o=1))
+        for bank in range(1, STACK_BANKS):
+            load_stack(bank)
 
         ident_f32 = keep.tile([P, P], F32)
         masks.make_identity(nc, ident_f32[:])
         ident_bf16 = keep.tile([P, P], BF16)
         masks.make_identity(nc, ident_bf16[:])
 
-        rows = keep.tile([P, DEPTH + 2, P], F32)
-        nc.gpsimd.memset(rows[:, DEPTH + 1, :], -1.0)
-        step = keep.tile([P, STEPS, P], F32)
-
         grouped = keep.tile([P, OPERANDS, P, PACK], BF16, align_bytes=64)
         grouped_words = grouped[:].bitcast(F32)
         codes = keep.tile([P, OPERANDS * P], U32, align_bytes=64)
         scales = keep.tile([P, OPERANDS * P], U8, align_bytes=64)
 
-        def turn_pair(pair):
-            turned = psum.tile([P, 2, HALVES, P], F32, tag="bank")
-            for i in range(2):
-                words = operands[:, 2 * pair + i, :].bitcast(F32)
+        def turn_operands(first, count):
+            turned = psum.tile([P, count, HALVES, P], F32, tag="bank", name="turned%d" % first)
+            for i in range(count):
+                words = operands[:, first + i, :].bitcast(F32)
                 for u in range(HALVES):
                     nc.tensor.transpose(
                         out=turned[:, i, u, :], in_=words[:, u : HALVES * P : HALVES], identity=ident_f32[:]
                     )
-            copy_out = nc.scalar.copy if pair % 2 == 0 else nc.vector.tensor_copy
+            return turned
+
+        def lay_out(copy_out, turned, first, count):
             copy_out(
-                out=grouped_words[:, 2 * pair : 2 * pair + 2, :, :],
+                out=grouped_words[:, first : first + count, :, :],
                 in_=turned[:].rearrange("p i u r -> p i r u"),
             )
 
-        def quantise_pair(pair):
-            cols = slice(2 * pair * P, (2 * pair + 2) * P)
+        def quantise(first, count):
+            cols = slice(first * P, (first + count) * P)
             nc.vector.quantize_mx(
                 out=codes[:, cols].bitcast(FP8X4),
                 scales=scales[:, cols],
-                in_=grouped[:, 2 * pair : 2 * pair + 2, :, :].rearrange("p o r t -> p (o r t)"),
+                in_=grouped[:, first : first + count, :, :].rearrange("p o r t -> p (o r t)"),
             )
 
-        turn_pair(0)
-        turn_pair(1)
-        quantise_pair(0)
-        bias_turned = psum.tile([P, P], BF16, tag="bank")
-        nc.tensor.transpose(out=bias_turned[:], in_=bias_rows[:], identity=ident_bf16[:])
-        bias = keep.tile([P, OUT + 1], F32)
-        nc.vector.tensor_copy(out=bias[:], in_=bias_turned[:, 0 : OUT + 1])
-        half_bs = keep.tile([P, 1], F32)
-        nc.vector.tensor_scalar_mul(out=half_bs[:], in0=bias[:, TOP : TOP + 1], scalar1=0.5)
-        quantise_pair(1)
-        turn_pair(2)
-        quantise_pair(2)
-
-        gates = psum.tile([P, TOP + 1, P], F32, tag="bank")
-        readout = psum.tile([P, P], F32, tag="bank")
         h_cols = slice(H_BLOCK * P, (H_BLOCK + 1) * P)
-        for j in range(OUT + 1):
+
+        def multiply(j, out):
             w_cols = slice((1 + j) * P, (2 + j) * P)
             nc.tensor.matmul_mx(
-                out=readout[:] if j == OUT else gates[:, j, :],
+                out=out,
                 lhsT=codes[:, w_cols].bitcast(FP8X4),
                 lhsT_scale=scales[:, w_cols],
                 rhs=codes[:, h_cols].bitcast(FP8X4),
@@ -125,67 +115,58 @@ def tile_stackrnn_pb_s_kernel(tc, h, stack, Wa, ba, Ws, bs, Wo, bo, out_0, out_1
                 stop=True,
             )
 
-        half_tanh = keep.tile([P, P], F32)
-        nc.scalar.activation(
-            out=half_tanh[:], in_=gates[:, TOP, :], func=ACT.Tanh, bias=half_bs[:], scale=0.5
-        )
-        nc.scalar.activation(out=rows[:, 0, :], in_=half_tanh[:], func=ACT.Copy, bias=0.5, scale=0.5)
-        out_turned = keep.tile([P, P], F32)
-        nc.scalar.activation(
-            out=out_turned[:], in_=readout[:], func=ACT.Identity, bias=bias[:, OUT : OUT + 1]
-        )
+        idle = psum.tile([P, HALVES, P], F32, tag="bank")
+        for i in range(WARM_UP):
+            nc.tensor.transpose(out=idle[:, 0, :], in_=ident_f32[:], identity=ident_f32[:])
 
-        stack_turned = []
-        for bank in range(STACK_BANKS):
-            turned_bank = psum.tile([P, SLICES_PER_BANK, P], BF16, tag="bank", name="stack_turned%d" % bank)
-            for i in range(SLICES_PER_BANK):
+        turned = [turn_operands(i, 1) for i in range(4)]
+        ba_turned = psum.tile([P, 3, P], BF16, tag="bank")
+        for j in (PUSH, POP, NOOP):
+            nc.tensor.transpose(out=ba_turned[:, j, :], in_=ba_rows[:, j, :], identity=ident_bf16[:])
+        lay_out(nc.scalar.copy, turned[0], 0, 1)
+        lay_out(nc.vector.tensor_copy, turned[1], 1, 1)
+        quantise(0, 2)
+        lay_out(nc.scalar.copy, turned[2], 2, 1)
+        lay_out(nc.vector.tensor_copy, turned[3], 3, 1)
+        quantise(2, 2)
+        ba_cols = keep.tile([P, 3], F32)
+        nc.vector.tensor_copy(out=ba_cols[:], in_=ba_turned[:, :, 0])
+
+        stack_turned = [None] * STACK_BANKS
+        stack_copy = keep.tile([P, DEPTH, P], BF16)
+
+        def turn_stack(first, count):
+            bank = first // BANK_ROWS
+            if first % BANK_ROWS == 0:
+                stack_turned[bank] = psum.tile([P, BANK_ROWS, P], BF16, tag="bank", name="stack_turned%d" % bank)
+            for d in range(first, first + count):
                 nc.tensor.transpose(
-                    out=turned_bank[:, i, :],
-                    in_=stack_sb[:, bank * SLICES_PER_BANK + i, :],
-                    identity=ident_bf16[:],
-                )
-            stack_turned.append(turned_bank)
-
-        def widen_bank(bank):
-            first = 1 + bank * SLICES_PER_BANK
-            nc.scalar.copy(out=rows[:, first : first + SLICES_PER_BANK, :], in_=stack_turned[bank][:])
-
-        def make_steps(piece):
-            lo = piece * CHUNK
-            hi = min(lo + CHUNK, STEPS)
-            nc.vector.tensor_sub(out=step[:, lo:hi, :], in0=rows[:, lo + 1 : hi + 1, :], in1=rows[:, lo:hi, :])
-
-        out_bank = psum.tile([P, P], F32, tag="bank")
-        nc.tensor.transpose(out=out_bank[:], in_=out_turned[:], identity=ident_f32[:])
-
-        chunks = [(first, CHUNK) for first in range(0, DEPTH - CHUNK, CHUNK)]
-        chunks += [(DEPTH - CHUNK, TAIL), (DEPTH - TAIL, TAIL)]
-        blended = []
-
-        def turn_back(bank, term, first_of_group, last_of_group):
-            count = term.shape[1]
-            for i in range(count):
-                nc.tensor.matmul(
-                    out=bank[:, i, :],
-                    lhsT=term[:, i, :],
-                    rhs=ident_f32[:],
-                    is_transpose=True,
-                    start=(first_of_group and i == 0),
-                    stop=(last_of_group and i == count - 1),
+                    out=stack_turned[bank][:, d % BANK_ROWS, :], in_=stack_sb[:, d, :], identity=ident_bf16[:]
                 )
 
-        def open_chunk(n):
-            first, count = chunks[n]
-            blended.append(psum.tile([P, count, P], F32, tag="bank", name="blended%d" % n))
-            turn_back(blended[n], rows[:, first + 1 : first + 1 + count, :], True, False)
+        def copy_stack(first, count):
+            bank_rows = slice(first % BANK_ROWS, first % BANK_ROWS + count)
+            nc.scalar.copy(out=stack_copy[:, first : first + count, :], in_=stack_turned[first // BANK_ROWS][:, bank_rows, :])
+
+        gates = psum.tile([P, NOOP + 1, P], F32, tag="bank")
+        multiply(PUSH, gates[:, PUSH, :])
+        ws_wo = turn_operands(1 + TOP, 2)
+        lay_out(nc.scalar.copy, ws_wo, 1 + TOP, 2)
+        multiply(POP, gates[:, POP, :])
+        multiply(NOOP, gates[:, NOOP, :])
+        turn_stack(0, BANK_ROWS)
+        copy_stack(0, GROUP)
+        bso_turned = psum.tile([P, P], BF16, tag="bank")
+        nc.tensor.transpose(out=bso_turned[:], in_=bso_rows[:], identity=ident_bf16[:])
+        turn_stack(BANK_ROWS, BANK_ROWS)
 
         halves = (slice(0, P // 2), slice(P // 2, P))
         logits = keep.tile([P, 3, P], F32)
         for cols in halves:
             nc.vector.tensor_tensor(
                 out=logits[:, :, cols],
-                in0=gates[:, PUSH : NOOP + 1, cols],
-                in1=bias[:, PUSH : NOOP + 1].unsqueeze(2).to_broadcast([P, 3, P // 2]),
+                in0=gates[:, :, cols],
+                in1=ba_cols[:].unsqueeze(2).to_broadcast([P, 3, P // 2]),
                 op=ALU.add,
             )
         peak = keep.tile([P, P], F32)
@@ -200,21 +181,17 @@ def tile_stackrnn_pb_s_kernel(tc, h, stack, Wa, ba, Ws, bs, Wo, bo, out_0, out_1
                 in1=peak[:, cols].unsqueeze(1).to_broadcast([P, 3, P // 2]),
                 op=ALU.subtract,
             )
-        widen_bank(0)
         raised = keep.tile([P, 3, P], F32)
         for cols in halves:
             nc.scalar.activation(out=raised[:, :, cols], in_=logits[:, :, cols], func=ACT.Exp)
-        widen_bank(1)
-        out_sb = keep.tile([P, P], F32)
-        nc.scalar.copy(out=out_sb[:], in_=out_bank[:])
-        nc.sync.dma_start(out=out_0, in_=out_sb[:])
-        widen_bank(2)
-        widen_bank(3)
-        for n in range(AHEAD):
-            open_chunk(n)
-
-        make_steps(0)
-        make_steps(1)
+        quantise(1 + TOP, 2)
+        half_bs = keep.tile([P, 1], F32)
+        nc.vector.tensor_scalar_mul(out=half_bs[:], in0=bso_turned[:, 0:1], scalar1=0.5)
+        bo_col = keep.tile([P, 1], F32)
+        nc.vector.tensor_copy(out=bo_col[:], in_=bso_turned[:, 1:2])
+        top_out = psum.tile([P, 2, P], F32, tag="bank")
+        multiply(TOP, top_out[:, 0, :])
+        multiply(OUT, top_out[:, 1, :])
         total = keep.tile([P, P], F32)
         for cols in halves:
             nc.vector.tensor_reduce(
@@ -222,42 +199,105 @@ def tile_stackrnn_pb_s_kernel(tc, h, stack, Wa, ba, Ws, bs, Wo, bo, out_0, out_1
             )
         for cols in halves:
             nc.vector.reciprocal(out=total[:, cols], in_=total[:, cols])
-        minus_push = keep.tile([P, P], F32)
+        act = keep.tile([P, 3, P], F32)
         for cols in halves:
-            nc.vector.scalar_tensor_tensor(
-                out=minus_push[:, cols],
-                in0=raised[:, PUSH, cols],
-                scalar=-1.0,
-                in1=total[:, cols],
-                op0=ALU.mult,
-                op1=ALU.mult,
+            nc.vector.tensor_tensor(
+                out=act[:, :, cols],
+                in0=raised[:, :, cols],
+                in1=total[:, cols].unsqueeze(1).to_broadcast([P, 3, P // 2]),
+                op=ALU.mult,
             )
-        pop = keep.tile([P, P], F32)
-        for cols in halves:
-            nc.vector.tensor_mul(out=pop[:, cols], in0=raised[:, POP, cols], in1=total[:, cols])
+        turn_stack(2 * BANK_ROWS, BANK_ROWS)
+        turn_stack(3 * BANK_ROWS, BANK_ROWS)
 
-        pushed = keep.tile([P, DEPTH, P], F32)
-        popped = keep.tile([P, DEPTH, P], F32)
+        copy_stack(GROUP, GROUP)
+        half_tanh = keep.tile([P, P], F32)
+        nc.scalar.activation(out=half_tanh[:], in_=top_out[:, 0, :], func=ACT.Tanh, bias=half_bs[:], scale=0.5)
+        top = keep.tile([P, P], F32)
+        nc.scalar.activation(out=top[:], in_=half_tanh[:], func=ACT.Copy, bias=0.5, scale=0.5)
+        out_turned = keep.tile([P, P], F32)
+        nc.scalar.activation(
+            out=out_turned[:], in_=top_out[:, 1, :], func=ACT.Identity, bias=bo_col[:]
+        )
+        copy_stack(BANK_ROWS, BANK_ROWS)
+
+        product = keep.tile([P, 3, DEPTH, P], F32)
+        edge = keep.tile([P, 2, P], F32)
+        nc.vector.tensor_mul(out=edge[:, PUSH, :], in0=top[:], in1=act[:, PUSH, :])
+        nc.scalar.mul(out=edge[:, POP, :], in_=act[:, POP, :], mul=-1.0)
+
+        bank_of = {}
+
+        def open_chunk(first, count):
+            tile = psum.tile([P, count, P], F32, tag="bank", name="blended%d" % first)
+            for i in range(count):
+                bank_of[first + i] = (tile, i)
+            return tile
+
+        opened = set()
+
+        def add_term(action, row, last_of_group=False):
+            source = row + {PUSH: -1, NOOP: 0, POP: 1}[action]
+            term = product[:, action, source, :] if 0 <= source < DEPTH else edge[:, action, :]
+            tile, i = bank_of[row]
+            key = row - i
+            nc.tensor.matmul(
+                out=tile[:, i, :],
+                lhsT=term,
+                rhs=ident_f32[:],
+                is_transpose=True,
+                start=key not in opened,
+                stop=last_of_group,
+            )
+            opened.add(key)
+
+        def finish(copy_out, first, count):
+            new_rows = staging.tile([P, count, P], F32, tag="new_rows", name="new_rows%d" % first)
+            copy_out(out=new_rows[:], in_=bank_of[first][0][:])
+            nc.sync.dma_start(out=out_1[:, first : first + count, :], in_=new_rows[:])
+
+        def multiply_rows(engine, source, actions, first, count):
+            n_actions = actions.stop - actions.start
+            engine.tensor_tensor(
+                out=product[:, actions, first : first + count, :],
+                in0=source.unsqueeze(1).to_broadcast([P, n_actions, count, P]),
+                in1=act[:, actions, :].unsqueeze(2).to_broadcast([P, n_actions, count, P]),
+                op=ALU.mult,
+            )
+
+        half = GROUP // 2
+        chunks = [(0, half), (half, half)]
+        chunks += [(first, GROUP) for first in range(GROUP, DEPTH - GROUP, GROUP)]
+        chunks += [(DEPTH - GROUP, half), (DEPTH - half, half)]
         for n, (first, count) in enumerate(chunks):
-            d_range = slice(first, first + count)
-            if (n + 2) * CHUNK < STEPS:
-                make_steps(n + 2)
-            nc.vector.tensor_tensor(
-                out=pushed[:, d_range, :],
-                in0=step[:, d_range, :],
-                in1=minus_push[:].unsqueeze(1).to_broadcast([P, count, P]),
-                op=ALU.mult,
-            )
-            nc.vector.tensor_tensor(
-                out=popped[:, d_range, :],
-                in0=step[:, first + 1 : first + 1 + count, :],
-                in1=pop[:].unsqueeze(1).to_broadcast([P, count, P]),
-                op=ALU.mult,
-            )
-            turn_back(blended[n], pushed[:, d_range, :], False, False)
-            turn_back(blended[n], popped[:, d_range, :], False, True)
-            if n + AHEAD < len(chunks):
-                open_chunk(n + AHEAD)
-            new_rows = staging.tile([P, count, P], F32, tag="new_rows")
-            nc.scalar.copy(out=new_rows[:], in_=blended[n][:])
-            nc.sync.dma_start(out=out_1[:, d_range, :], in_=new_rows[:])
+            bank_rows = slice(first % BANK_ROWS, first % BANK_ROWS + count)
+            source = stack_turned[first // BANK_ROWS][:, bank_rows, :]
+            if first < DEPTH - GROUP:
+                multiply_rows(
+                    nc.gpsimd, stack_copy[:, first : first + count, :], slice(NOOP, NOOP + 1), first, count
+                )
+                multiply_rows(nc.vector, source, slice(PUSH, POP + 1), first, count)
+            else:
+                multiply_rows(nc.vector, source, slice(PUSH, NOOP + 1), first, count)
+            if n > 0:
+                before = chunks[n - 1]
+                add_term(POP, first - 1, last_of_group=True)
+                finish(nc.scalar.copy, before[0], before[1])
+            open_chunk(first, count)
+            for row in range(first, first + count - 1):
+                add_term(POP, row)
+            for row in range(first, first + count):
+                add_term(PUSH, row)
+            for row in range(first, first + count):
+                add_term(NOOP, row)
+            if n == 2:
+                copy_stack(2 * BANK_ROWS, BANK_ROWS)
+                out_bank = psum.tile([P, P], F32, tag="bank")
+                nc.tensor.transpose(out=out_bank[:], in_=out_turned[:], identity=ident_f32[:])
+            if n == 3:
+                copy_stack(3 * BANK_ROWS, GROUP)
+                out_sb = keep.tile([P, P], F32)
+                nc.scalar.copy(out=out_sb[:], in_=out_bank[:])
+                nc.sync.dma_start(out=out_0, in_=out_sb[:])
+        add_term(POP, DEPTH - 1, last_of_group=True)
+        finish(nc.vector.tensor_copy, DEPTH - GROUP // 2, GROUP // 2)

@@ -26,6 +26,7 @@ PSUM_BANKS = 8
 BANK_ROWS = 8
 STACK_BANKS = DEPTH // BANK_ROWS
 GROUP = 4
+KICK = 4
 WARM_UP = 8
 
 FLOPS = 2 * P * HDIM * (3 * P + P + P)
@@ -209,6 +210,17 @@ def tile_stackrnn_pb_s_kernel(tc, h, stack, Wa, ba, Ws, bs, Wo, bo, out_0, out_1
             )
         turn_stack(2 * BANK_ROWS, BANK_ROWS)
         turn_stack(3 * BANK_ROWS, BANK_ROWS)
+        spare = psum.tile([P, 4 * P], F32, tag="bank")
+        for i in range(KICK):
+            nc.tensor.matmul_mx(
+                out=spare[:],
+                lhsT=codes[:, 0:P].bitcast(FP8X4),
+                lhsT_scale=scales[:, 0:P],
+                rhs=codes[:, 0 : 4 * P].bitcast(FP8X4),
+                rhs_scale=scales[:, 0 : 4 * P],
+                start=True,
+                stop=True,
+            )
 
         copy_stack(GROUP, GROUP)
         half_tanh = keep.tile([P, P], F32)

@@ -10,7 +10,6 @@ U8 = mybir.dt.uint8
 FP8X4 = mybir.dt.float8_e4m3fn_x4
 ACT = mybir.ActivationFunctionType
 ALU = mybir.AluOpType
-AXIS = mybir.AxisListType
 
 P = 128
 HDIM = 512
@@ -26,6 +25,8 @@ PSUM_BANKS = 8
 BANK_ROWS = 8
 STACK_BANKS = DEPTH // BANK_ROWS
 GROUP = 4
+FIRST_SPARE = 2
+GPSIMD_ROWS = range(4, 26)
 KICK = 4
 WARM_UP = 8
 
@@ -36,8 +37,9 @@ def tile_stackrnn_pb_s_kernel(tc, h, stack, Wa, ba, Ws, bs, Wo, bo, out_0, out_1
     nc = tc.nc
     with ExitStack() as ctx:
         keep = ctx.enter_context(tc.tile_pool(name="keep", bufs=1))
-        staging = ctx.enter_context(tc.tile_pool(name="staging", bufs=4))
-        psum = ctx.enter_context(tc.psum_pool(name="psum", bufs=PSUM_BANKS))
+        staging = ctx.enter_context(tc.tile_pool(name="staging", bufs=8))
+        psum = ctx.enter_context(tc.psum_pool(name="psum", bufs=PSUM_BANKS - 1))
+        late = ctx.enter_context(tc.psum_pool(name="late", bufs=1))
         ctx.enter_context(tc.manual_schedule())
 
         ba_rows = keep.tile([P, 3, P], BF16)
@@ -128,76 +130,83 @@ def tile_stackrnn_pb_s_kernel(tc, h, stack, Wa, ba, Ws, bs, Wo, bo, out_0, out_1
         lay_out(nc.vector.tensor_copy, turned[1], 1, 1)
         quantise(0, 2)
         lay_out(nc.scalar.copy, turned[2], 2, 1)
-        lay_out(nc.vector.tensor_copy, turned[3], 3, 1)
-        quantise(2, 2)
+        quantise(2, 1)
+        lay_out(nc.scalar.copy, turned[3], 3, 1)
+        quantise(3, 1)
         ba_cols = keep.tile([P, 3], F32)
-        nc.vector.tensor_copy(out=ba_cols[:], in_=ba_turned[:, :, 0])
+        nc.scalar.copy(out=ba_cols[:], in_=ba_turned[:, :, 0])
 
         stack_turned = [None] * STACK_BANKS
         stack_copy = keep.tile([P, DEPTH, P], BF16)
 
-        def turn_stack(first, count):
-            bank = first // BANK_ROWS
-            if first % BANK_ROWS == 0:
-                stack_turned[bank] = psum.tile([P, BANK_ROWS, P], BF16, tag="bank", name="stack_turned%d" % bank)
-            for d in range(first, first + count):
+        def turn_stack(bank):
+            stack_turned[bank] = psum.tile([P, BANK_ROWS, P], BF16, tag="bank", name="stack_turned%d" % bank)
+            for i in range(BANK_ROWS):
                 nc.tensor.transpose(
-                    out=stack_turned[bank][:, d % BANK_ROWS, :], in_=stack_sb[:, d, :], identity=ident_bf16[:]
+                    out=stack_turned[bank][:, i, :], in_=stack_sb[:, bank * BANK_ROWS + i, :], identity=ident_bf16[:]
                 )
 
         def copy_stack(first, count):
             bank_rows = slice(first % BANK_ROWS, first % BANK_ROWS + count)
             nc.scalar.copy(out=stack_copy[:, first : first + count, :], in_=stack_turned[first // BANK_ROWS][:, bank_rows, :])
 
-        gates = psum.tile([P, NOOP + 1, P], F32, tag="bank")
-        multiply(PUSH, gates[:, PUSH, :])
-        ws_wo = turn_operands(1 + TOP, 2)
-        lay_out(nc.scalar.copy, ws_wo, 1 + TOP, 2)
-        multiply(POP, gates[:, POP, :])
-        multiply(NOOP, gates[:, NOOP, :])
-        turn_stack(0, BANK_ROWS)
-        copy_stack(0, GROUP)
+        def spare_passes(tile, count):
+            for i in range(count):
+                nc.tensor.matmul_mx(
+                    out=tile[:],
+                    lhsT=codes[:, 0:P].bitcast(FP8X4),
+                    lhsT_scale=scales[:, 0:P],
+                    rhs=codes[:, 0 : 4 * P].bitcast(FP8X4),
+                    rhs_scale=scales[:, 0 : 4 * P],
+                    start=True,
+                    stop=True,
+                )
+
+        gates_ab = psum.tile([P, 2, P], F32, tag="bank")
+        gates_c = psum.tile([P, P], F32, tag="bank")
+        gate = {PUSH: gates_ab[:, PUSH, :], POP: gates_ab[:, POP, :], NOOP: gates_c[:]}
+        for j in (PUSH, POP, NOOP):
+            multiply(j, gate[j])
+        ws_turned = turn_operands(1 + TOP, 1)
         bso_turned = psum.tile([P, P], BF16, tag="bank")
         nc.tensor.transpose(out=bso_turned[:], in_=bso_rows[:], identity=ident_bf16[:])
-        turn_stack(BANK_ROWS, BANK_ROWS)
-
-        halves = (slice(0, P // 2), slice(P // 2, P))
-        logits = keep.tile([P, 3, P], F32)
-        for cols in halves:
-            nc.vector.tensor_tensor(
-                out=logits[:, :, cols],
-                in0=gates[:, :, cols],
-                in1=ba_cols[:].unsqueeze(2).to_broadcast([P, 3, P // 2]),
-                op=ALU.add,
-            )
-        peak = keep.tile([P, P], F32)
-        for cols in halves:
-            nc.vector.tensor_reduce(
-                out=peak[:, cols], in_=logits[:, :, cols].rearrange("p j b -> p b j"), axis=AXIS.X, op=ALU.max
-            )
-        for cols in halves:
-            nc.vector.tensor_tensor(
-                out=logits[:, :, cols],
-                in0=logits[:, :, cols],
-                in1=peak[:, cols].unsqueeze(1).to_broadcast([P, 3, P // 2]),
-                op=ALU.subtract,
-            )
-        raised = keep.tile([P, 3, P], F32)
-        for cols in halves:
-            nc.scalar.activation(out=raised[:, :, cols], in_=logits[:, :, cols], func=ACT.Exp)
-        quantise(1 + TOP, 2)
+        first_spare = psum.tile([P, 4 * P], F32, tag="bank")
+        spare_passes(first_spare, FIRST_SPARE)
+        turn_stack(0)
+        turn_stack(1)
+        lay_out(nc.scalar.copy, ws_turned, 1 + TOP, 1)
         half_bs = keep.tile([P, 1], F32)
-        nc.vector.tensor_scalar_mul(out=half_bs[:], in0=bso_turned[:, 0:1], scalar1=0.5)
+        nc.scalar.mul(out=half_bs[:], in_=bso_turned[:, 0:1], mul=0.5)
         bo_col = keep.tile([P, 1], F32)
-        nc.vector.tensor_copy(out=bo_col[:], in_=bso_turned[:, 1:2])
-        top_out = psum.tile([P, 2, P], F32, tag="bank")
-        multiply(TOP, top_out[:, 0, :])
-        multiply(OUT, top_out[:, 1, :])
+        nc.scalar.copy(out=bo_col[:], in_=bso_turned[:, 1:2])
+
+        def with_bias(out, j, other, op):
+            nc.vector.scalar_tensor_tensor(
+                out=out, in0=gate[j], scalar=ba_cols[:, j : j + 1], in1=other, op0=ALU.add, op1=op
+            )
+
+        pop_logit = keep.tile([P, P], F32)
+        nc.vector.tensor_scalar_add(out=pop_logit[:], in0=gate[POP], scalar1=ba_cols[:, POP : POP + 1])
+        higher = keep.tile([P, P], F32)
+        with_bias(higher[:], PUSH, pop_logit[:], ALU.max)
+        peak = keep.tile([P, P], F32)
+        with_bias(peak[:], NOOP, higher[:], ALU.max)
+        below = keep.tile([P, 3, P], F32)
+        raised = keep.tile([P, 3, P], F32)
+        for j in (PUSH, POP, NOOP):
+            with_bias(below[:, j, :], j, peak[:], ALU.subtract)
+            nc.scalar.activation(out=raised[:, j, :], in_=below[:, j, :], func=ACT.Exp)
+        quantise(1 + TOP, 1)
+        top_bank = late.tile([P, P], F32, tag="late")
+        multiply(TOP, top_bank[:])
+        turn_stack(2)
+        halves = (slice(0, P // 2), slice(P // 2, P))
+        half = GROUP // 2
         total = keep.tile([P, P], F32)
         for cols in halves:
-            nc.vector.tensor_reduce(
-                out=total[:, cols], in_=raised[:, :, cols].rearrange("p j b -> p b j"), axis=AXIS.X, op=ALU.add
-            )
+            nc.vector.tensor_add(out=total[:, cols], in0=raised[:, PUSH, cols], in1=raised[:, POP, cols])
+        for cols in halves:
+            nc.vector.tensor_add(out=total[:, cols], in0=total[:, cols], in1=raised[:, NOOP, cols])
         for cols in halves:
             nc.vector.reciprocal(out=total[:, cols], in_=total[:, cols])
         act = keep.tile([P, 3, P], F32)
@@ -208,35 +217,20 @@ def tile_stackrnn_pb_s_kernel(tc, h, stack, Wa, ba, Ws, bs, Wo, bo, out_0, out_1
                 in1=total[:, cols].unsqueeze(1).to_broadcast([P, 3, P // 2]),
                 op=ALU.mult,
             )
-        turn_stack(2 * BANK_ROWS, BANK_ROWS)
-        turn_stack(3 * BANK_ROWS, BANK_ROWS)
-        spare = psum.tile([P, 4 * P], F32, tag="bank")
-        for i in range(KICK):
-            nc.tensor.matmul_mx(
-                out=spare[:],
-                lhsT=codes[:, 0:P].bitcast(FP8X4),
-                lhsT_scale=scales[:, 0:P],
-                rhs=codes[:, 0 : 4 * P].bitcast(FP8X4),
-                rhs_scale=scales[:, 0 : 4 * P],
-                start=True,
-                stop=True,
-            )
-
-        copy_stack(GROUP, GROUP)
         half_tanh = keep.tile([P, P], F32)
-        nc.scalar.activation(out=half_tanh[:], in_=top_out[:, 0, :], func=ACT.Tanh, bias=half_bs[:], scale=0.5)
+        nc.scalar.activation(out=half_tanh[:], in_=top_bank[:], func=ACT.Tanh, bias=half_bs[:], scale=0.5)
+        copy_stack(GROUP, GROUP)
         top = keep.tile([P, P], F32)
         nc.scalar.activation(out=top[:], in_=half_tanh[:], func=ACT.Copy, bias=0.5, scale=0.5)
-        out_turned = keep.tile([P, P], F32)
-        nc.scalar.activation(
-            out=out_turned[:], in_=top_out[:, 1, :], func=ACT.Identity, bias=bo_col[:]
-        )
         copy_stack(BANK_ROWS, BANK_ROWS)
+        copy_stack(2 * BANK_ROWS, BANK_ROWS)
+        spare = late.tile([P, 4 * P], F32, tag="late")
+        spare_passes(spare, KICK)
+        turn_stack(3)
+        copy_stack(3 * BANK_ROWS, half)
 
         product = keep.tile([P, 3, DEPTH, P], F32)
         edge = keep.tile([P, 2, P], F32)
-        nc.vector.tensor_mul(out=edge[:, PUSH, :], in0=top[:], in1=act[:, PUSH, :])
-        nc.scalar.mul(out=edge[:, POP, :], in_=act[:, POP, :], mul=-1.0)
 
         bank_of = {}
 
@@ -244,7 +238,6 @@ def tile_stackrnn_pb_s_kernel(tc, h, stack, Wa, ba, Ws, bs, Wo, bo, out_0, out_1
             tile = psum.tile([P, count, P], F32, tag="bank", name="blended%d" % first)
             for i in range(count):
                 bank_of[first + i] = (tile, i)
-            return tile
 
         opened = set()
 
@@ -268,48 +261,72 @@ def tile_stackrnn_pb_s_kernel(tc, h, stack, Wa, ba, Ws, bs, Wo, bo, out_0, out_1
             copy_out(out=new_rows[:], in_=bank_of[first][0][:])
             nc.sync.dma_start(out=out_1[:, first : first + count, :], in_=new_rows[:])
 
-        def multiply_rows(engine, source, actions, first, count):
+        def multiply_rows(engine, actions, first, count, cols=slice(0, P)):
+            if engine is nc.gpsimd:
+                source = stack_copy[:, first : first + count, cols]
+            else:
+                start = first % BANK_ROWS
+                source = stack_turned[first // BANK_ROWS][:, start : start + count, cols]
             n_actions = actions.stop - actions.start
+            width = cols.stop - cols.start
             engine.tensor_tensor(
-                out=product[:, actions, first : first + count, :],
-                in0=source.unsqueeze(1).to_broadcast([P, n_actions, count, P]),
-                in1=act[:, actions, :].unsqueeze(2).to_broadcast([P, n_actions, count, P]),
+                out=product[:, actions, first : first + count, cols],
+                in0=source.unsqueeze(1).to_broadcast([P, n_actions, count, width]),
+                in1=act[:, actions, cols].unsqueeze(2).to_broadcast([P, n_actions, count, width]),
                 op=ALU.mult,
             )
 
-        half = GROUP // 2
         chunks = [(0, half), (half, half)]
-        chunks += [(first, GROUP) for first in range(GROUP, DEPTH - GROUP, GROUP)]
-        chunks += [(DEPTH - GROUP, half), (DEPTH - half, half)]
+        chunks += [(first, GROUP) for first in range(GROUP, DEPTH - 2 * GROUP, GROUP)]
+        chunks += [(first, half) for first in range(DEPTH - 2 * GROUP, DEPTH, half)]
+        last = len(chunks) - 1
         for n, (first, count) in enumerate(chunks):
-            bank_rows = slice(first % BANK_ROWS, first % BANK_ROWS + count)
-            source = stack_turned[first // BANK_ROWS][:, bank_rows, :]
-            if first < DEPTH - GROUP:
-                multiply_rows(
-                    nc.gpsimd, stack_copy[:, first : first + count, :], slice(NOOP, NOOP + 1), first, count
-                )
-                multiply_rows(nc.vector, source, slice(PUSH, POP + 1), first, count)
+            if n == 0:
+                for cols in halves:
+                    multiply_rows(nc.vector, slice(PUSH, NOOP + 1), first, count, cols)
+            elif first in GPSIMD_ROWS:
+                multiply_rows(nc.gpsimd, slice(NOOP, NOOP + 1), first, count)
+                multiply_rows(nc.vector, slice(PUSH, POP + 1), first, count)
+            elif n < last:
+                multiply_rows(nc.vector, slice(PUSH, NOOP + 1), first, count)
             else:
-                multiply_rows(nc.vector, source, slice(PUSH, NOOP + 1), first, count)
+                multiply_rows(nc.vector, slice(PUSH, NOOP + 1), first, 1)
+                multiply_rows(nc.vector, slice(POP, NOOP + 1), first + 1, 1)
             if n > 0:
-                before = chunks[n - 1]
                 add_term(POP, first - 1, last_of_group=True)
-                finish(nc.scalar.copy, before[0], before[1])
+                finish(nc.scalar.copy, *chunks[n - 1])
             open_chunk(first, count)
+            if n == 0:
+                nc.gpsimd.tensor_tensor(out=edge[:, PUSH, :], in0=top[:], in1=act[:, PUSH, :], op=ALU.mult)
+                nc.scalar.mul(out=edge[:, POP, :], in_=act[:, POP, :], mul=-1.0)
+            if n == last:
+                add_term(PUSH, first)
+                add_term(NOOP, first)
+                add_term(PUSH, first + 1)
+                add_term(POP, first)
+                add_term(NOOP, first + 1)
+                add_term(POP, first + 1, last_of_group=True)
+                finish(nc.vector.tensor_copy, first, count)
+                continue
             for row in range(first, first + count - 1):
                 add_term(POP, row)
-            for row in range(first, first + count):
+            for row in reversed(range(first, first + count)):
                 add_term(PUSH, row)
             for row in range(first, first + count):
                 add_term(NOOP, row)
-            if n == 2:
-                copy_stack(2 * BANK_ROWS, BANK_ROWS)
+            if n == 1:
+                wo_turned = turn_operands(1 + OUT, 1)
+                lay_out(nc.scalar.copy, wo_turned, 1 + OUT, 1)
+            if n == 5:
+                quantise(1 + OUT, 1)
                 out_bank = psum.tile([P, P], F32, tag="bank")
-                nc.tensor.transpose(out=out_bank[:], in_=out_turned[:], identity=ident_f32[:])
-            if n == 3:
-                copy_stack(3 * BANK_ROWS, GROUP)
+                multiply(OUT, out_bank[:])
+                out_turned = keep.tile([P, P], F32)
+                nc.scalar.activation(out=out_turned[:], in_=out_bank[:], func=ACT.Identity, bias=bo_col[:])
+            if n == 7:
+                out_back = psum.tile([P, P], F32, tag="bank")
+                nc.tensor.transpose(out=out_back[:], in_=out_turned[:], identity=ident_f32[:])
+            if n == 8:
                 out_sb = keep.tile([P, P], F32)
-                nc.scalar.copy(out=out_sb[:], in_=out_bank[:])
+                nc.scalar.copy(out=out_sb[:], in_=out_back[:])
                 nc.sync.dma_start(out=out_0, in_=out_sb[:])
-        add_term(POP, DEPTH - 1, last_of_group=True)
-        finish(nc.vector.tensor_copy, DEPTH - GROUP // 2, GROUP // 2)

@@ -19,6 +19,7 @@ PACK = 4
 
 H_BLOCK = 0
 PUSH, POP, NOOP, TOP, OUT = 0, 1, 2, 3, 4
+SLOT = {POP: 1, PUSH: 2, NOOP: 3, TOP: 4, OUT: 5}
 OPERANDS = 6
 
 PSUM_BANKS = 8
@@ -27,7 +28,8 @@ STACK_BANKS = DEPTH // BANK_ROWS
 GROUP = 4
 FIRST_SPARE = 2
 GPSIMD_ROWS = range(4, 26)
-KICK = 4
+FILLERS, FILLER_COLUMNS = 7, 32
+KICK = 6
 WARM_UP = 8
 
 FLOPS = 2 * P * HDIM * (3 * P + P + P)
@@ -42,10 +44,8 @@ def tile_stackrnn_pb_s_kernel(tc, h, stack, Wa, ba, Ws, bs, Wo, bo, out_0, out_1
         late = ctx.enter_context(tc.psum_pool(name="late", bufs=1))
         ctx.enter_context(tc.manual_schedule())
 
-        ba_rows = keep.tile([P, 3, P], BF16)
-        nc.vector.memset(ba_rows[:], 0.0)
-        bso_rows = keep.tile([P, P], BF16)
-        nc.vector.memset(bso_rows[:], 0.0)
+        bias_rows = keep.tile([P, P], BF16)
+        nc.vector.memset(bias_rows[:], 0.0)
 
         warm = keep.tile([P, 1], F32)
         nc.vector.memset(warm[:], 0.0)
@@ -53,22 +53,23 @@ def tile_stackrnn_pb_s_kernel(tc, h, stack, Wa, ba, Ws, bs, Wo, bo, out_0, out_1
 
         operands = keep.tile([P, OPERANDS, HDIM], BF16)
         nc.sync.dma_start(out=operands[:, H_BLOCK, :], in_=h)
-        for j in (PUSH, POP, NOOP):
-            nc.sync.dma_start(out=operands[:, 1 + j, :], in_=Wa[j * P : (j + 1) * P, :])
-        nc.sync.dma_start(out=ba_rows[0:1, :, :], in_=ba.rearrange("(o j n) -> o j n", o=1, n=P))
-        nc.sync.dma_start(out=operands[:, 1 + TOP, :], in_=Ws)
-        nc.sync.dma_start(out=operands[:, 1 + OUT, :], in_=Wo)
+        for j in (POP, PUSH, NOOP):
+            nc.sync.dma_start(out=operands[:, SLOT[j], :], in_=Wa[j * P : (j + 1) * P, :])
+        action_bias = ba.rearrange("(j n) -> j n", n=P)
+        nc.sync.dma_start(out=bias_rows[PUSH : POP + 1, :], in_=action_bias[PUSH : POP + 1, :])
+        nc.sync.dma_start(out=bias_rows[NOOP : NOOP + 1, :], in_=action_bias[NOOP : NOOP + 1, :])
+        nc.sync.dma_start(out=bias_rows[TOP : TOP + 1, :], in_=bs.rearrange("(o n) -> o n", o=1))
+        nc.sync.dma_start(out=bias_rows[OUT : OUT + 1, :], in_=bo.rearrange("(o n) -> o n", o=1))
+        nc.sync.dma_start(out=operands[:, SLOT[TOP], :], in_=Ws)
         stack_sb = keep.tile([P, DEPTH, P], BF16)
 
         def load_stack(bank):
             d_range = slice(bank * BANK_ROWS, (bank + 1) * BANK_ROWS)
             nc.sync.dma_start(out=stack_sb[:, d_range, :], in_=stack[:, d_range, :])
 
-        load_stack(0)
-        nc.sync.dma_start(out=bso_rows[0:1, :], in_=bs.rearrange("(o n) -> o n", o=1))
-        nc.sync.dma_start(out=bso_rows[1:2, :], in_=bo.rearrange("(o n) -> o n", o=1))
-        for bank in range(1, STACK_BANKS):
+        for bank in range(STACK_BANKS):
             load_stack(bank)
+        nc.sync.dma_start(out=operands[:, SLOT[OUT], :], in_=Wo)
 
         ident_f32 = keep.tile([P, P], F32)
         masks.make_identity(nc, ident_f32[:])
@@ -107,7 +108,7 @@ def tile_stackrnn_pb_s_kernel(tc, h, stack, Wa, ba, Ws, bs, Wo, bo, out_0, out_1
         h_cols = slice(H_BLOCK * P, (H_BLOCK + 1) * P)
 
         def multiply(j, out):
-            w_cols = slice((1 + j) * P, (2 + j) * P)
+            w_cols = slice(SLOT[j] * P, (SLOT[j] + 1) * P)
             nc.tensor.matmul_mx(
                 out=out,
                 lhsT=codes[:, w_cols].bitcast(FP8X4),
@@ -123,9 +124,8 @@ def tile_stackrnn_pb_s_kernel(tc, h, stack, Wa, ba, Ws, bs, Wo, bo, out_0, out_1
             nc.tensor.transpose(out=idle[:, 0, :], in_=ident_f32[:], identity=ident_f32[:])
 
         turned = [turn_operands(i, 1) for i in range(4)]
-        ba_turned = psum.tile([P, 3, P], BF16, tag="bank")
-        for j in (PUSH, POP, NOOP):
-            nc.tensor.transpose(out=ba_turned[:, j, :], in_=ba_rows[:, j, :], identity=ident_bf16[:])
+        bias_turned = late.tile([P, P], BF16, tag="late")
+        nc.tensor.transpose(out=bias_turned[:], in_=bias_rows[:], identity=ident_bf16[:])
         lay_out(nc.scalar.copy, turned[0], 0, 1)
         lay_out(nc.vector.tensor_copy, turned[1], 1, 1)
         quantise(0, 2)
@@ -134,7 +134,9 @@ def tile_stackrnn_pb_s_kernel(tc, h, stack, Wa, ba, Ws, bs, Wo, bo, out_0, out_1
         lay_out(nc.scalar.copy, turned[3], 3, 1)
         quantise(3, 1)
         ba_cols = keep.tile([P, 3], F32)
-        nc.scalar.copy(out=ba_cols[:], in_=ba_turned[:, :, 0])
+        nc.scalar.copy(out=ba_cols[:], in_=bias_turned[:, PUSH : NOOP + 1])
+        half_bs = keep.tile([P, 1], F32)
+        nc.scalar.mul(out=half_bs[:], in_=bias_turned[:, TOP : TOP + 1], mul=0.5)
 
         stack_turned = [None] * STACK_BANKS
         stack_copy = keep.tile([P, DEPTH, P], BF16)
@@ -165,20 +167,14 @@ def tile_stackrnn_pb_s_kernel(tc, h, stack, Wa, ba, Ws, bs, Wo, bo, out_0, out_1
         gates_ab = psum.tile([P, 2, P], F32, tag="bank")
         gates_c = psum.tile([P, P], F32, tag="bank")
         gate = {PUSH: gates_ab[:, PUSH, :], POP: gates_ab[:, POP, :], NOOP: gates_c[:]}
-        for j in (PUSH, POP, NOOP):
+        for j in (POP, PUSH, NOOP):
             multiply(j, gate[j])
-        ws_turned = turn_operands(1 + TOP, 1)
-        bso_turned = psum.tile([P, P], BF16, tag="bank")
-        nc.tensor.transpose(out=bso_turned[:], in_=bso_rows[:], identity=ident_bf16[:])
+        ws_turned = turn_operands(SLOT[TOP], 1)
         first_spare = psum.tile([P, 4 * P], F32, tag="bank")
         spare_passes(first_spare, FIRST_SPARE)
         turn_stack(0)
         turn_stack(1)
-        lay_out(nc.scalar.copy, ws_turned, 1 + TOP, 1)
-        half_bs = keep.tile([P, 1], F32)
-        nc.scalar.mul(out=half_bs[:], in_=bso_turned[:, 0:1], mul=0.5)
-        bo_col = keep.tile([P, 1], F32)
-        nc.scalar.copy(out=bo_col[:], in_=bso_turned[:, 1:2])
+        lay_out(nc.scalar.copy, ws_turned, SLOT[TOP], 1)
 
         def with_bias(out, j, other, op):
             nc.vector.scalar_tensor_tensor(
@@ -196,8 +192,8 @@ def tile_stackrnn_pb_s_kernel(tc, h, stack, Wa, ba, Ws, bs, Wo, bo, out_0, out_1
         for j in (PUSH, POP, NOOP):
             with_bias(below[:, j, :], j, peak[:], ALU.subtract)
             nc.scalar.activation(out=raised[:, j, :], in_=below[:, j, :], func=ACT.Exp)
-        quantise(1 + TOP, 1)
-        top_bank = late.tile([P, P], F32, tag="late")
+        quantise(SLOT[TOP], 1)
+        top_bank = psum.tile([P, P], F32, tag="bank")
         multiply(TOP, top_bank[:])
         turn_stack(2)
         halves = (slice(0, P // 2), slice(P // 2, P))
@@ -207,6 +203,8 @@ def tile_stackrnn_pb_s_kernel(tc, h, stack, Wa, ba, Ws, bs, Wo, bo, out_0, out_1
             nc.vector.tensor_add(out=total[:, cols], in0=raised[:, PUSH, cols], in1=raised[:, POP, cols])
         for cols in halves:
             nc.vector.tensor_add(out=total[:, cols], in0=total[:, cols], in1=raised[:, NOOP, cols])
+        bo_col = keep.tile([P, 1], F32)
+        nc.vector.tensor_copy(out=bo_col[:], in_=bias_turned[:, OUT : OUT + 1])
         for cols in halves:
             nc.vector.reciprocal(out=total[:, cols], in_=total[:, cols])
         act = keep.tile([P, 3, P], F32)
@@ -314,11 +312,19 @@ def tile_stackrnn_pb_s_kernel(tc, h, stack, Wa, ba, Ws, bs, Wo, bo, out_0, out_1
                 add_term(PUSH, row)
             for row in range(first, first + count):
                 add_term(NOOP, row)
+            if n < FILLERS:
+                nc.tensor.matmul(
+                    out=spare[:, 0:FILLER_COLUMNS],
+                    lhsT=ident_f32[:],
+                    rhs=ident_f32[:, 0:FILLER_COLUMNS],
+                    start=True,
+                    stop=True,
+                )
             if n == 1:
-                wo_turned = turn_operands(1 + OUT, 1)
-                lay_out(nc.scalar.copy, wo_turned, 1 + OUT, 1)
+                wo_turned = turn_operands(SLOT[OUT], 1)
+                lay_out(nc.scalar.copy, wo_turned, SLOT[OUT], 1)
             if n == 5:
-                quantise(1 + OUT, 1)
+                quantise(SLOT[OUT], 1)
                 out_bank = psum.tile([P, P], F32, tag="bank")
                 multiply(OUT, out_bank[:])
                 out_turned = keep.tile([P, P], F32)

@@ -26,10 +26,9 @@ PSUM_BANKS = 8
 BANK_ROWS = 8
 STACK_BANKS = DEPTH // BANK_ROWS
 GROUP = 4
-FIRST_SPARE = 2
+FIRST_SPARE = 4
 GPSIMD_ROWS = range(4, 26)
-FILLERS, FILLER_COLUMNS = 7, 32
-KICK = 6
+KICK = 8
 WARM_UP = 8
 
 FLOPS = 2 * P * HDIM * (3 * P + P + P)
@@ -61,6 +60,7 @@ def tile_stackrnn_pb_s_kernel(tc, h, stack, Wa, ba, Ws, bs, Wo, bo, out_0, out_1
         nc.sync.dma_start(out=bias_rows[TOP : TOP + 1, :], in_=bs.rearrange("(o n) -> o n", o=1))
         nc.sync.dma_start(out=bias_rows[OUT : OUT + 1, :], in_=bo.rearrange("(o n) -> o n", o=1))
         nc.sync.dma_start(out=operands[:, SLOT[TOP], :], in_=Ws)
+        nc.sync.dma_start(out=operands[:, SLOT[OUT], :], in_=Wo)
         stack_sb = keep.tile([P, DEPTH, P], BF16)
 
         def load_stack(bank):
@@ -69,7 +69,6 @@ def tile_stackrnn_pb_s_kernel(tc, h, stack, Wa, ba, Ws, bs, Wo, bo, out_0, out_1
 
         for bank in range(STACK_BANKS):
             load_stack(bank)
-        nc.sync.dma_start(out=operands[:, SLOT[OUT], :], in_=Wo)
 
         ident_f32 = keep.tile([P, P], F32)
         masks.make_identity(nc, ident_f32[:])
@@ -170,11 +169,13 @@ def tile_stackrnn_pb_s_kernel(tc, h, stack, Wa, ba, Ws, bs, Wo, bo, out_0, out_1
         for j in (POP, PUSH, NOOP):
             multiply(j, gate[j])
         ws_turned = turn_operands(SLOT[TOP], 1)
+        wo_turned = turn_operands(SLOT[OUT], 1)
         first_spare = psum.tile([P, 4 * P], F32, tag="bank")
         spare_passes(first_spare, FIRST_SPARE)
         turn_stack(0)
         turn_stack(1)
         lay_out(nc.scalar.copy, ws_turned, SLOT[TOP], 1)
+        lay_out(nc.scalar.copy, wo_turned, SLOT[OUT], 1)
 
         def with_bias(out, j, other, op):
             nc.vector.scalar_tensor_tensor(
@@ -192,9 +193,11 @@ def tile_stackrnn_pb_s_kernel(tc, h, stack, Wa, ba, Ws, bs, Wo, bo, out_0, out_1
         for j in (PUSH, POP, NOOP):
             with_bias(below[:, j, :], j, peak[:], ALU.subtract)
             nc.scalar.activation(out=raised[:, j, :], in_=below[:, j, :], func=ACT.Exp)
-        quantise(SLOT[TOP], 1)
+        quantise(SLOT[TOP], 2)
         top_bank = psum.tile([P, P], F32, tag="bank")
         multiply(TOP, top_bank[:])
+        out_bank = psum.tile([P, P], F32, tag="bank")
+        multiply(OUT, out_bank[:])
         turn_stack(2)
         halves = (slice(0, P // 2), slice(P // 2, P))
         half = GROUP // 2
@@ -217,6 +220,8 @@ def tile_stackrnn_pb_s_kernel(tc, h, stack, Wa, ba, Ws, bs, Wo, bo, out_0, out_1
             )
         half_tanh = keep.tile([P, P], F32)
         nc.scalar.activation(out=half_tanh[:], in_=top_bank[:], func=ACT.Tanh, bias=half_bs[:], scale=0.5)
+        out_turned = keep.tile([P, P], F32)
+        nc.scalar.activation(out=out_turned[:], in_=out_bank[:], func=ACT.Identity, bias=bo_col[:])
         copy_stack(GROUP, GROUP)
         top = keep.tile([P, P], F32)
         nc.scalar.activation(out=top[:], in_=half_tanh[:], func=ACT.Copy, bias=0.5, scale=0.5)
@@ -225,7 +230,12 @@ def tile_stackrnn_pb_s_kernel(tc, h, stack, Wa, ba, Ws, bs, Wo, bo, out_0, out_1
         spare = late.tile([P, 4 * P], F32, tag="late")
         spare_passes(spare, KICK)
         turn_stack(3)
+        out_back = psum.tile([P, P], F32, tag="bank")
+        nc.tensor.transpose(out=out_back[:], in_=out_turned[:], identity=ident_f32[:])
         copy_stack(3 * BANK_ROWS, half)
+        out_sb = keep.tile([P, P], F32)
+        nc.scalar.copy(out=out_sb[:], in_=out_back[:])
+        nc.sync.dma_start(out=out_0, in_=out_sb[:])
 
         product = keep.tile([P, 3, DEPTH, P], F32)
         edge = keep.tile([P, 2, P], F32)
@@ -269,8 +279,8 @@ def tile_stackrnn_pb_s_kernel(tc, h, stack, Wa, ba, Ws, bs, Wo, bo, out_0, out_1
             width = cols.stop - cols.start
             engine.tensor_tensor(
                 out=product[:, actions, first : first + count, cols],
-                in0=source.unsqueeze(1).to_broadcast([P, n_actions, count, width]),
-                in1=act[:, actions, cols].unsqueeze(2).to_broadcast([P, n_actions, count, width]),
+                in0=act[:, actions, cols].unsqueeze(2).to_broadcast([P, n_actions, count, width]),
+                in1=source.unsqueeze(1).to_broadcast([P, n_actions, count, width]),
                 op=ALU.mult,
             )
 
@@ -312,27 +322,3 @@ def tile_stackrnn_pb_s_kernel(tc, h, stack, Wa, ba, Ws, bs, Wo, bo, out_0, out_1
                 add_term(PUSH, row)
             for row in range(first, first + count):
                 add_term(NOOP, row)
-            if n < FILLERS:
-                nc.tensor.matmul(
-                    out=spare[:, 0:FILLER_COLUMNS],
-                    lhsT=ident_f32[:],
-                    rhs=ident_f32[:, 0:FILLER_COLUMNS],
-                    start=True,
-                    stop=True,
-                )
-            if n == 1:
-                wo_turned = turn_operands(SLOT[OUT], 1)
-                lay_out(nc.scalar.copy, wo_turned, SLOT[OUT], 1)
-            if n == 5:
-                quantise(SLOT[OUT], 1)
-                out_bank = psum.tile([P, P], F32, tag="bank")
-                multiply(OUT, out_bank[:])
-                out_turned = keep.tile([P, P], F32)
-                nc.scalar.activation(out=out_turned[:], in_=out_bank[:], func=ACT.Identity, bias=bo_col[:])
-            if n == 7:
-                out_back = psum.tile([P, P], F32, tag="bank")
-                nc.tensor.transpose(out=out_back[:], in_=out_turned[:], identity=ident_f32[:])
-            if n == 8:
-                out_sb = keep.tile([P, P], F32)
-                nc.scalar.copy(out=out_sb[:], in_=out_back[:])
-                nc.sync.dma_start(out=out_0, in_=out_sb[:])

@@ -27,8 +27,9 @@ BANK_ROWS = 8
 STACK_BANKS = DEPTH // BANK_ROWS
 GROUP = 4
 FIRST_SPARE = 4
-GPSIMD_ROWS = range(4, 26)
-KICK = 8
+GPSIMD_ROWS = range(4, 30)
+FILLERS, FILLER_COLUMNS = (2, 4, 6), 80
+KICK = 6
 WARM_UP = 8
 
 FLOPS = 2 * P * HDIM * (3 * P + P + P)
@@ -232,7 +233,7 @@ def tile_stackrnn_pb_s_kernel(tc, h, stack, Wa, ba, Ws, bs, Wo, bo, out_0, out_1
         turn_stack(3)
         out_back = psum.tile([P, P], F32, tag="bank")
         nc.tensor.transpose(out=out_back[:], in_=out_turned[:], identity=ident_f32[:])
-        copy_stack(3 * BANK_ROWS, half)
+        copy_stack(3 * BANK_ROWS, 3 * half)
         out_sb = keep.tile([P, P], F32)
         nc.scalar.copy(out=out_sb[:], in_=out_back[:])
         nc.sync.dma_start(out=out_0, in_=out_sb[:])
@@ -322,3 +323,11 @@ def tile_stackrnn_pb_s_kernel(tc, h, stack, Wa, ba, Ws, bs, Wo, bo, out_0, out_1
                 add_term(PUSH, row)
             for row in range(first, first + count):
                 add_term(NOOP, row)
+            if n in FILLERS:
+                nc.tensor.matmul(
+                    out=spare[:, 0:FILLER_COLUMNS],
+                    lhsT=ident_f32[:],
+                    rhs=ident_f32[:, 0:FILLER_COLUMNS],
+                    start=True,
+                    stop=True,
+                )

@@ -26,8 +26,8 @@ PSUM_BANKS = 8
 BANK_ROWS = 8
 STACK_BANKS = DEPTH // BANK_ROWS
 GROUP = 4
-FIRST_SPARE = 4
-GPSIMD_ROWS = range(4, 30)
+FIRST_SPARE = 3
+GPSIMD_ROWS = range(2, 30)
 FILLERS, FILLER_COLUMNS = (2, 4, 6), 80
 KICK = 6
 WARM_UP = 8
@@ -178,21 +178,31 @@ def tile_stackrnn_pb_s_kernel(tc, h, stack, Wa, ba, Ws, bs, Wo, bo, out_0, out_1
         lay_out(nc.scalar.copy, ws_turned, SLOT[TOP], 1)
         lay_out(nc.scalar.copy, wo_turned, SLOT[OUT], 1)
 
-        def with_bias(out, j, other, op):
+        halves = (slice(0, P // 2), slice(P // 2, P))
+
+        def with_bias(out, j, other, op, cols=slice(0, P)):
             nc.vector.scalar_tensor_tensor(
-                out=out, in0=gate[j], scalar=ba_cols[:, j : j + 1], in1=other, op0=ALU.add, op1=op
+                out=out[:, cols],
+                in0=gate[j][:, cols],
+                scalar=ba_cols[:, j : j + 1],
+                in1=other[:, cols],
+                op0=ALU.add,
+                op1=op,
             )
 
         pop_logit = keep.tile([P, P], F32)
-        nc.vector.tensor_scalar_add(out=pop_logit[:], in0=gate[POP], scalar1=ba_cols[:, POP : POP + 1])
+        for cols in halves:
+            nc.vector.tensor_scalar_add(out=pop_logit[:, cols], in0=gate[POP][:, cols], scalar1=ba_cols[:, POP : POP + 1])
         higher = keep.tile([P, P], F32)
-        with_bias(higher[:], PUSH, pop_logit[:], ALU.max)
+        for cols in halves:
+            with_bias(higher, PUSH, pop_logit, ALU.max, cols)
         peak = keep.tile([P, P], F32)
-        with_bias(peak[:], NOOP, higher[:], ALU.max)
+        for cols in halves:
+            with_bias(peak, NOOP, higher, ALU.max, cols)
         below = keep.tile([P, 3, P], F32)
         raised = keep.tile([P, 3, P], F32)
         for j in (PUSH, POP, NOOP):
-            with_bias(below[:, j, :], j, peak[:], ALU.subtract)
+            with_bias(below[:, j, :], j, peak, ALU.subtract)
             nc.scalar.activation(out=raised[:, j, :], in_=below[:, j, :], func=ACT.Exp)
         quantise(SLOT[TOP], 2)
         top_bank = psum.tile([P, P], F32, tag="bank")
@@ -200,7 +210,6 @@ def tile_stackrnn_pb_s_kernel(tc, h, stack, Wa, ba, Ws, bs, Wo, bo, out_0, out_1
         out_bank = psum.tile([P, P], F32, tag="bank")
         multiply(OUT, out_bank[:])
         turn_stack(2)
-        halves = (slice(0, P // 2), slice(P // 2, P))
         half = GROUP // 2
         total = keep.tile([P, P], F32)
         for cols in halves:
@@ -223,14 +232,14 @@ def tile_stackrnn_pb_s_kernel(tc, h, stack, Wa, ba, Ws, bs, Wo, bo, out_0, out_1
         nc.scalar.activation(out=half_tanh[:], in_=top_bank[:], func=ACT.Tanh, bias=half_bs[:], scale=0.5)
         out_turned = keep.tile([P, P], F32)
         nc.scalar.activation(out=out_turned[:], in_=out_bank[:], func=ACT.Identity, bias=bo_col[:])
-        copy_stack(GROUP, GROUP)
+        copy_stack(half, 3 * half)
         top = keep.tile([P, P], F32)
         nc.scalar.activation(out=top[:], in_=half_tanh[:], func=ACT.Copy, bias=0.5, scale=0.5)
         copy_stack(BANK_ROWS, BANK_ROWS)
         copy_stack(2 * BANK_ROWS, BANK_ROWS)
+        turn_stack(3)
         spare = late.tile([P, 4 * P], F32, tag="late")
         spare_passes(spare, KICK)
-        turn_stack(3)
         out_back = psum.tile([P, P], F32, tag="bank")
         nc.tensor.transpose(out=out_back[:], in_=out_turned[:], identity=ident_f32[:])
         copy_stack(3 * BANK_ROWS, 3 * half)

@@ -26,10 +26,10 @@ PSUM_BANKS = 8
 BANK_ROWS = 8
 STACK_BANKS = DEPTH // BANK_ROWS
 GROUP = 4
-FIRST_SPARE = 3
+FIRST_SPARE = 2
 GPSIMD_ROWS = range(2, 30)
-FILLERS, FILLER_COLUMNS = (2, 4, 6), 80
-KICK = 6
+FILLERS, FILLER_COLUMNS = (1, 3, 5, 7), 60
+KICK = 5
 WARM_UP = 8
 
 FLOPS = 2 * P * HDIM * (3 * P + P + P)
@@ -296,7 +296,8 @@ def tile_stackrnn_pb_s_kernel(tc, h, stack, Wa, ba, Ws, bs, Wo, bo, out_0, out_1
 
         chunks = [(0, half), (half, half)]
         chunks += [(first, GROUP) for first in range(GROUP, DEPTH - 2 * GROUP, GROUP)]
-        chunks += [(first, half) for first in range(DEPTH - 2 * GROUP, DEPTH, half)]
+        chunks += [(first, half) for first in range(DEPTH - 2 * GROUP, DEPTH - half, half)]
+        chunks += [(DEPTH - 2, 1), (DEPTH - 1, 1)]
         last = len(chunks) - 1
         for n, (first, count) in enumerate(chunks):
             if n == 0:
@@ -308,8 +309,7 @@ def tile_stackrnn_pb_s_kernel(tc, h, stack, Wa, ba, Ws, bs, Wo, bo, out_0, out_1
             elif n < last:
                 multiply_rows(nc.vector, slice(PUSH, NOOP + 1), first, count)
             else:
-                multiply_rows(nc.vector, slice(PUSH, NOOP + 1), first, 1)
-                multiply_rows(nc.vector, slice(POP, NOOP + 1), first + 1, 1)
+                multiply_rows(nc.vector, slice(POP, NOOP + 1), first, count)
             if n > 0:
                 add_term(POP, first - 1, last_of_group=True)
                 finish(nc.scalar.copy, *chunks[n - 1])
@@ -319,11 +319,8 @@ def tile_stackrnn_pb_s_kernel(tc, h, stack, Wa, ba, Ws, bs, Wo, bo, out_0, out_1
                 nc.scalar.mul(out=edge[:, POP, :], in_=act[:, POP, :], mul=-1.0)
             if n == last:
                 add_term(PUSH, first)
-                add_term(NOOP, first)
-                add_term(PUSH, first + 1)
                 add_term(POP, first)
-                add_term(NOOP, first + 1)
-                add_term(POP, first + 1, last_of_group=True)
+                add_term(NOOP, first, last_of_group=True)
                 finish(nc.vector.tensor_copy, first, count)
                 continue
             for row in range(first, first + count - 1):

from contextlib import ExitStack

import concourse.masks as masks
import concourse.mybir as mybir

F32 = mybir.dt.float32
BF16 = mybir.dt.bfloat16
U32 = mybir.dt.uint32
U8 = mybir.dt.uint8
FP8X4 = mybir.dt.float8_e4m3fn_x4
ACT = mybir.ActivationFunctionType
ALU = mybir.AluOpType

P = 128
HDIM = 512
DEPTH = 32
HALVES = 2
PACK = 4

H_BLOCK = 0
PUSH, POP, NOOP, TOP, OUT = 0, 1, 2, 3, 4
SLOT = {POP: 1, PUSH: 2, NOOP: 3, TOP: 4, OUT: 5}
OPERANDS = 6

PSUM_BANKS = 8
BANK_ROWS = 8
STACK_BANKS = DEPTH // BANK_ROWS
GROUP = 4
FIRST_SPARE = 2
GPSIMD_ROWS = range(2, 30)
FILLERS, FILLER_COLUMNS = (1, 3, 5, 7), 60
KICK = 5
WARM_UP = 8

FLOPS = 2 * P * HDIM * (3 * P + P + P)


def tile_stackrnn_pb_s_kernel(tc, h, stack, Wa, ba, Ws, bs, Wo, bo, out_0, out_1):
    nc = tc.nc
    with ExitStack() as ctx:
        keep = ctx.enter_context(tc.tile_pool(name="keep", bufs=1))
        staging = ctx.enter_context(tc.tile_pool(name="staging", bufs=8))
        psum = ctx.enter_context(tc.psum_pool(name="psum", bufs=PSUM_BANKS - 1))
        late = ctx.enter_context(tc.psum_pool(name="late", bufs=1))
        ctx.enter_context(tc.manual_schedule())

        bias_rows = keep.tile([P, P], BF16)
        nc.vector.memset(bias_rows[:], 0.0)

        warm = keep.tile([P, 1], F32)
        nc.vector.memset(warm[:], 0.0)
        nc.scalar.activation(out=warm[:], in_=warm[:], func=ACT.Exp)

        operands = keep.tile([P, OPERANDS, HDIM], BF16)
        nc.sync.dma_start(out=operands[:, H_BLOCK, :], in_=h)
        for j in (POP, PUSH, NOOP):
            nc.sync.dma_start(out=operands[:, SLOT[j], :], in_=Wa[j * P : (j + 1) * P, :])
        action_bias = ba.rearrange("(j n) -> j n", n=P)
        nc.sync.dma_start(out=bias_rows[PUSH : POP + 1, :], in_=action_bias[PUSH : POP + 1, :])
        nc.sync.dma_start(out=bias_rows[NOOP : NOOP + 1, :], in_=action_bias[NOOP : NOOP + 1, :])
        nc.sync.dma_start(out=bias_rows[TOP : TOP + 1, :], in_=bs.rearrange("(o n) -> o n", o=1))
        nc.sync.dma_start(out=bias_rows[OUT : OUT + 1, :], in_=bo.rearrange("(o n) -> o n", o=1))
        nc.sync.dma_start(out=operands[:, SLOT[TOP], :], in_=Ws)
        nc.sync.dma_start(out=operands[:, SLOT[OUT], :], in_=Wo)
        stack_sb = keep.tile([P, DEPTH, P], BF16)

        def load_stack(bank):
            d_range = slice(bank * BANK_ROWS, (bank + 1) * BANK_ROWS)
            nc.sync.dma_start(out=stack_sb[:, d_range, :], in_=stack[:, d_range, :])

        for bank in range(STACK_BANKS):
            load_stack(bank)

        ident_f32 = keep.tile([P, P], F32)
        masks.make_identity(nc, ident_f32[:])
        ident_bf16 = keep.tile([P, P], BF16)
        masks.make_identity(nc, ident_bf16[:])

        grouped = keep.tile([P, OPERANDS, P, PACK], BF16, align_bytes=64)
        grouped_words = grouped[:].bitcast(F32)
        codes = keep.tile([P, OPERANDS * P], U32, align_bytes=64)
        scales = keep.tile([P, OPERANDS * P], U8, align_bytes=64)

        def turn_operands(first, count):
            turned = psum.tile([P, count, HALVES, P], F32, tag="bank", name="turned%d" % first)
            for i in range(count):
                words = operands[:, first + i, :].bitcast(F32)
                for u in range(HALVES):
                    nc.tensor.transpose(
                        out=turned[:, i, u, :], in_=words[:, u : HALVES * P : HALVES], identity=ident_f32[:]
                    )
            return turned

        def lay_out(copy_out, turned, first, count):
            copy_out(
                out=grouped_words[:, first : first + count, :, :],
                in_=turned[:].rearrange("p i u r -> p i r u"),
            )

        def quantise(first, count):
            cols = slice(first * P, (first + count) * P)
            nc.vector.quantize_mx(
                out=codes[:, cols].bitcast(FP8X4),
                scales=scales[:, cols],
                in_=grouped[:, first : first + count, :, :].rearrange("p o r t -> p (o r t)"),
            )

        h_cols = slice(H_BLOCK * P, (H_BLOCK + 1) * P)

        def multiply(j, out):
            w_cols = slice(SLOT[j] * P, (SLOT[j] + 1) * P)
            nc.tensor.matmul_mx(
                out=out,
                lhsT=codes[:, w_cols].bitcast(FP8X4),
                lhsT_scale=scales[:, w_cols],
                rhs=codes[:, h_cols].bitcast(FP8X4),
                rhs_scale=scales[:, h_cols],
                start=True,
                stop=True,
            )

        idle = psum.tile([P, HALVES, P], F32, tag="bank")
        for i in range(WARM_UP):
            nc.tensor.transpose(out=idle[:, 0, :], in_=ident_f32[:], identity=ident_f32[:])

        turned = [turn_operands(i, 1) for i in range(4)]
        bias_turned = late.tile([P, P], BF16, tag="late")
        nc.tensor.transpose(out=bias_turned[:], in_=bias_rows[:], identity=ident_bf16[:])
        lay_out(nc.scalar.copy, turned[0], 0, 1)
        lay_out(nc.vector.tensor_copy, turned[1], 1, 1)
        quantise(0, 2)
        lay_out(nc.scalar.copy, turned[2], 2, 1)
        quantise(2, 1)
        lay_out(nc.scalar.copy, turned[3], 3, 1)
        quantise(3, 1)
        ba_cols = keep.tile([P, 3], F32)
        nc.scalar.copy(out=ba_cols[:], in_=bias_turned[:, PUSH : NOOP + 1])
        half_bs = keep.tile([P, 1], F32)
        nc.scalar.mul(out=half_bs[:], in_=bias_turned[:, TOP : TOP + 1], mul=0.5)

        stack_turned = [None] * STACK_BANKS
        stack_copy = keep.tile([P, DEPTH, P], BF16)

        def turn_stack(bank):
            stack_turned[bank] = psum.tile([P, BANK_ROWS, P], BF16, tag="bank", name="stack_turned%d" % bank)
            for i in range(BANK_ROWS):
                nc.tensor.transpose(
                    out=stack_turned[bank][:, i, :], in_=stack_sb[:, bank * BANK_ROWS + i, :], identity=ident_bf16[:]
                )

        def copy_stack(first, count):
            bank_rows = slice(first % BANK_ROWS, first % BANK_ROWS + count)
            nc.scalar.copy(out=stack_copy[:, first : first + count, :], in_=stack_turned[first // BANK_ROWS][:, bank_rows, :])

        def spare_passes(tile, count):
            for i in range(count):
                nc.tensor.matmul_mx(
                    out=tile[:],
                    lhsT=codes[:, 0:P].bitcast(FP8X4),
                    lhsT_scale=scales[:, 0:P],
                    rhs=codes[:, 0 : 4 * P].bitcast(FP8X4),
                    rhs_scale=scales[:, 0 : 4 * P],
                    start=True,
                    stop=True,
                )

        gates_ab = psum.tile([P, 2, P], F32, tag="bank")
        gates_c = psum.tile([P, P], F32, tag="bank")
        gate = {PUSH: gates_ab[:, PUSH, :], POP: gates_ab[:, POP, :], NOOP: gates_c[:]}
        for j in (POP, PUSH, NOOP):
            multiply(j, gate[j])
        ws_turned = turn_operands(SLOT[TOP], 1)
        wo_turned = turn_operands(SLOT[OUT], 1)
        first_spare = psum.tile([P, 4 * P], F32, tag="bank")
        spare_passes(first_spare, FIRST_SPARE)
        turn_stack(0)
        turn_stack(1)
        lay_out(nc.scalar.copy, ws_turned, SLOT[TOP], 1)
        lay_out(nc.scalar.copy, wo_turned, SLOT[OUT], 1)

        halves = (slice(0, P // 2), slice(P // 2, P))

        def with_bias(out, j, other, op, cols=slice(0, P)):
            nc.vector.scalar_tensor_tensor(
                out=out[:, cols],
                in0=gate[j][:, cols],
                scalar=ba_cols[:, j : j + 1],
                in1=other[:, cols],
                op0=ALU.add,
                op1=op,
            )

        pop_logit = keep.tile([P, P], F32)
        for cols in halves:
            nc.vector.tensor_scalar_add(out=pop_logit[:, cols], in0=gate[POP][:, cols], scalar1=ba_cols[:, POP : POP + 1])
        higher = keep.tile([P, P], F32)
        for cols in halves:
            with_bias(higher, PUSH, pop_logit, ALU.max, cols)
        peak = keep.tile([P, P], F32)
        for cols in halves:
            with_bias(peak, NOOP, higher, ALU.max, cols)
        below = keep.tile([P, 3, P], F32)
        raised = keep.tile([P, 3, P], F32)
        for j in (PUSH, POP, NOOP):
            with_bias(below[:, j, :], j, peak, ALU.subtract)
            nc.scalar.activation(out=raised[:, j, :], in_=below[:, j, :], func=ACT.Exp)
        quantise(SLOT[TOP], 2)
        top_bank = psum.tile([P, P], F32, tag="bank")
        multiply(TOP, top_bank[:])
        out_bank = psum.tile([P, P], F32, tag="bank")
        multiply(OUT, out_bank[:])
        turn_stack(2)
        half = GROUP // 2
        total = keep.tile([P, P], F32)
        for cols in halves:
            nc.vector.tensor_add(out=total[:, cols], in0=raised[:, PUSH, cols], in1=raised[:, POP, cols])
        for cols in halves:
            nc.vector.tensor_add(out=total[:, cols], in0=total[:, cols], in1=raised[:, NOOP, cols])
        bo_col = keep.tile([P, 1], F32)
        nc.vector.tensor_copy(out=bo_col[:], in_=bias_turned[:, OUT : OUT + 1])
        for cols in halves:
            nc.vector.reciprocal(out=total[:, cols], in_=total[:, cols])
        act = keep.tile([P, 3, P], F32)
        for cols in halves:
            nc.vector.tensor_tensor(
                out=act[:, :, cols],
                in0=raised[:, :, cols],
                in1=total[:, cols].unsqueeze(1).to_broadcast([P, 3, P // 2]),
                op=ALU.mult,
            )
        half_tanh = keep.tile([P, P], F32)
        nc.scalar.activation(out=half_tanh[:], in_=top_bank[:], func=ACT.Tanh, bias=half_bs[:], scale=0.5)
        out_turned = keep.tile([P, P], F32)
        nc.scalar.activation(out=out_turned[:], in_=out_bank[:], func=ACT.Identity, bias=bo_col[:])
        copy_stack(half, 3 * half)
        top = keep.tile([P, P], F32)
        nc.scalar.activation(out=top[:], in_=half_tanh[:], func=ACT.Copy, bias=0.5, scale=0.5)
        copy_stack(BANK_ROWS, BANK_ROWS)
        copy_stack(2 * BANK_ROWS, BANK_ROWS)
        turn_stack(3)
        spare = late.tile([P, 4 * P], F32, tag="late")
        spare_passes(spare, KICK)
        out_back = psum.tile([P, P], F32, tag="bank")
        nc.tensor.transpose(out=out_back[:], in_=out_turned[:], identity=ident_f32[:])
        copy_stack(3 * BANK_ROWS, 3 * half)
        out_sb = keep.tile([P, P], F32)
        nc.scalar.copy(out=out_sb[:], in_=out_back[:])
        nc.sync.dma_start(out=out_0, in_=out_sb[:])

        product = keep.tile([P, 3, DEPTH, P], F32)
        edge = keep.tile([P, 2, P], F32)

        bank_of = {}

        def open_chunk(first, count):
            tile = psum.tile([P, count, P], F32, tag="bank", name="blended%d" % first)
            for i in range(count):
                bank_of[first + i] = (tile, i)

        opened = set()

        def add_term(action, row, last_of_group=False):
            source = row + {PUSH: -1, NOOP: 0, POP: 1}[action]
            term = product[:, action, source, :] if 0 <= source < DEPTH else edge[:, action, :]
            tile, i = bank_of[row]
            key = row - i
            nc.tensor.matmul(
                out=tile[:, i, :],
                lhsT=term,
                rhs=ident_f32[:],
                is_transpose=True,
                start=key not in opened,
                stop=last_of_group,
            )
            opened.add(key)

        def finish(copy_out, first, count):
            new_rows = staging.tile([P, count, P], F32, tag="new_rows", name="new_rows%d" % first)
            copy_out(out=new_rows[:], in_=bank_of[first][0][:])
            nc.sync.dma_start(out=out_1[:, first : first + count, :], in_=new_rows[:])

        def multiply_rows(engine, actions, first, count, cols=slice(0, P)):
            if engine is nc.gpsimd:
                source = stack_copy[:, first : first + count, cols]
            else:
                start = first % BANK_ROWS
                source = stack_turned[first // BANK_ROWS][:, start : start + count, cols]
            n_actions = actions.stop - actions.start
            width = cols.stop - cols.start
            engine.tensor_tensor(
                out=product[:, actions, first : first + count, cols],
                in0=act[:, actions, cols].unsqueeze(2).to_broadcast([P, n_actions, count, width]),
                in1=source.unsqueeze(1).to_broadcast([P, n_actions, count, width]),
                op=ALU.mult,
            )

        chunks = [(0, half), (half, half)]
        chunks += [(first, GROUP) for first in range(GROUP, DEPTH - 2 * GROUP, GROUP)]
        chunks += [(first, half) for first in range(DEPTH - 2 * GROUP, DEPTH - half, half)]
        chunks += [(DEPTH - 2, 1), (DEPTH - 1, 1)]
        last = len(chunks) - 1
        for n, (first, count) in enumerate(chunks):
            if n == 0:
                for cols in halves:
                    multiply_rows(nc.vector, slice(PUSH, NOOP + 1), first, count, cols)
            elif first in GPSIMD_ROWS:
                multiply_rows(nc.gpsimd, slice(NOOP, NOOP + 1), first, count)
                multiply_rows(nc.vector, slice(PUSH, POP + 1), first, count)
            elif n < last:
                multiply_rows(nc.vector, slice(PUSH, NOOP + 1), first, count)
            else:
                multiply_rows(nc.vector, slice(POP, NOOP + 1), first, count)
            if n > 0:
                add_term(POP, first - 1, last_of_group=True)
                finish(nc.scalar.copy, *chunks[n - 1])
            open_chunk(first, count)
            if n == 0:
                nc.gpsimd.tensor_tensor(out=edge[:, PUSH, :], in0=top[:], in1=act[:, PUSH, :], op=ALU.mult)
                nc.scalar.mul(out=edge[:, POP, :], in_=act[:, POP, :], mul=-1.0)
            if n == last:
                add_term(PUSH, first)
                add_term(POP, first)
                add_term(NOOP, first, last_of_group=True)
                finish(nc.vector.tensor_copy, first, count)
                continue
            for row in range(first, first + count - 1):
                add_term(POP, row)
            for row in reversed(range(first, first + count)):
                add_term(PUSH, row)
            for row in range(first, first + count):
                add_term(NOOP, row)
            if n in FILLERS:
                nc.tensor.matmul(
                    out=spare[:, 0:FILLER_COLUMNS],
                    lhsT=ident_f32[:],
                    rhs=ident_f32[:, 0:FILLER_COLUMNS],
                    start=True,
                    stop=True,
                )
